import numpy as np
import ml_dtypes


def mxq(x, axis, fmt="e4m3"):
    dtype, down = {"e4m3": (ml_dtypes.float8_e4m3fn, 7), "e5m2": (ml_dtypes.float8_e5m2, 14)}[fmt]
    v = np.moveaxis(np.asarray(x, np.float32).astype(ml_dtypes.bfloat16).astype(np.float64), axis, -1)
    blocks = v.reshape(v.shape[:-1] + (-1, 32))
    amax = np.abs(blocks).max(-1, keepdims=True)
    byte = np.maximum(np.where(amax > 0, np.frexp(amax)[1] - 1 + 127, 0) - down, 1)
    scale = np.exp2(byte - 127.0)
    codes = (blocks / scale).astype(np.float32).astype(dtype).astype(np.float64)
    return np.moveaxis((codes * scale).reshape(v.shape), -1, axis)


WIDE = False


def mx_kscale(k):
    if not WIDE:
        return np.ones(k)
    levels = np.array([10, -10, 5, -5, 0])
    a = np.random.permutation(np.resize(levels, k // 512 * 4)).reshape(k // 512, 4)
    idx = np.arange(k)
    return np.exp2(a[idx // 512, idx % 128 // 32])


BF16 = ml_dtypes.bfloat16


def bf(x):
    return np.asarray(x, np.float32).astype(BF16)


def f64(x):
    return np.asarray(x).astype(np.float64)


B, D, E, H, L = 128, 512, 8, 512, 32
NOISE_EPS = 0.01
MEAN_EPS = 1e-8


def softplus(z):
    return np.log(1.0 + np.exp(z))


def noisy_gates(clean_logits, noise_pre, noise):
    sd = softplus(noise_pre) + NOISE_EPS
    l = clean_logits + noise * sd
    e = np.exp(l - l.max(1, keepdims=True))
    p = e / e.sum(1, keepdims=True)
    m = p.mean(-1) - MEAN_EPS
    g = np.where(p >= m[:, None], p, 0.0)
    return g / g.sum(-1, keepdims=True)


def setup_inputs():
    s = mx_kscale(D)
    return {"x": bf(np.random.standard_normal((B, D)) * s),
            "noise": bf(np.random.standard_normal((B, E))),
            "clean_logits": bf(np.random.standard_normal((B, E))),
            "noise_pre": bf(np.random.standard_normal((B, E))),
            "W1": bf(np.random.standard_normal((E, D, H)) / np.sqrt(D) / s[None, :, None]),
            "b1": bf(np.random.standard_normal((E, H)) * 0.2),
            "W2": bf(np.random.standard_normal((E, H, L)) * 2.0 / np.sqrt(H)),
            "b2": bf(np.random.standard_normal((E, L)) * 0.3)}


def reference(x, noise, clean_logits, noise_pre, W1, b1, W2, b2):
    gates = noisy_gates(f64(clean_logits), f64(noise_pre), f64(noise))
    h = np.tanh((mxq(f64(x), 1, "e4m3") @ mxq(f64(W1), 1, "e4m3")) + f64(b1)[:, None, :])
    y = (mxq(h, 2, "e4m3") @ mxq(f64(W2), 1, "e4m3")) + f64(b2)[:, None, :]
    return gates[:, :, None] * y.transpose(1, 0, 2)

@@ -1,0 +1,227 @@
+from contextlib import ExitStack
+
+import concourse.mybir as mybir
+from concourse.masks import make_identity
+
+F32 = mybir.dt.float32
+BF16 = mybir.dt.bfloat16
+U32 = mybir.dt.uint32
+U8 = mybir.dt.uint8
+FP8X4 = mybir.dt.float8_e4m3fn_x4
+ACT = mybir.ActivationFunctionType
+ALU = mybir.AluOpType
+AX = mybir.AxisListType
+
+B, D, E, H, L = 128, 512, 8, 512, 32
+NOISE_EPS = 0.01
+MEAN_EPS = 1e-8
+
+P = 128
+PACK = 4
+E_HALF = 4
+RUN = 4
+VECTOR_COLS = 256
+
+FLOPS = 2 * B * D * H * E + 2 * B * H * L * E
+
+
+def regroup(copy, dst, src):
+    copy(
+        out=dst.rearrange("p (c i) j -> p c j i", i=RUN),
+        in_=src.rearrange("p j (c i) -> p c j i", i=RUN),
+    )
+
+
+def tile_mblfe_pa_s_kernel(tc, x, noise, clean_logits, noise_pre, W1, b1, W2, b2, out):
+    nc = tc.nc
+    with ExitStack() as ctx:
+        consts = ctx.enter_context(tc.tile_pool(name="consts", bufs=1))
+        w1_in = ctx.enter_context(tc.tile_pool(name="w1_in", bufs=E))
+        stage = ctx.enter_context(tc.tile_pool(name="stage", bufs=3))
+        psum_setup = ctx.enter_context(tc.psum_pool(name="psum_setup", bufs=1))
+        psum_h = ctx.enter_context(tc.psum_pool(name="psum_h", bufs=3))
+        psum_y = ctx.enter_context(tc.psum_pool(name="psum_y", bufs=2))
+
+        b1_rows = consts.tile([P, P], BF16)
+        nc.vector.memset(b1_rows[:], 0.0)
+        b2_row = consts.tile([P, E * L], BF16)
+        nc.vector.memset(b2_row[:], 0.0)
+        ones = consts.tile([P, P], BF16)
+        nc.vector.memset(ones[:], 1.0)
+        one_col = consts.tile([P, 1], F32)
+        nc.vector.memset(one_col[:], 1.0)
+
+        pre = consts.tile([B, E], BF16)
+        nc.scalar.dma_start(out=pre[:], in_=noise_pre)
+        eps_noise = consts.tile([B, E], BF16)
+        nc.scalar.dma_start(out=eps_noise[:], in_=noise)
+        clean = consts.tile([B, E], BF16)
+        nc.scalar.dma_start(out=clean[:], in_=clean_logits)
+        nc.scalar.dma_start(out=b1_rows[0 : E * PACK, :], in_=b1.rearrange("e (t p) -> (e t) p", p=P))
+        nc.scalar.dma_start(out=b2_row[0:1, :], in_=b2.rearrange("(o e) l -> o (e l)", o=1))
+
+        x_rows = consts.tile([B, D], BF16)
+        nc.sync.dma_start(out=x_rows[:], in_=x)
+        w1_raw = []
+        w2_raw = []
+        for e in range(E):
+            raw = w1_in.tile([P, PACK, H], BF16)
+            nc.sync.dma_start(out=raw[:], in_=W1[e].rearrange("(p j) h -> p j h", j=PACK))
+            w1_raw.append(raw)
+            if e % E_HALF == 1:
+                a = e // E_HALF
+                raw2 = consts.tile([P, E_HALF, PACK, L], BF16, name="w2_raw%d" % a)
+                nc.sync.dma_start(
+                    out=raw2[:],
+                    in_=W2[a * E_HALF : (a + 1) * E_HALF].rearrange("e (t p) l -> p e t l", p=P),
+                )
+                w2_raw.append(raw2)
+
+        ident = consts.tile([P, P], F32)
+        make_identity(nc, ident[:])
+        x_words = x_rows[:].bitcast(F32).rearrange("b (p u) -> b u p", u=2)
+        xT_ps = psum_setup.tile([P, 2, B], F32)
+        for u in range(2):
+            nc.tensor.transpose(xT_ps[:, u, :], x_words[:, u, :], ident[:])
+        x_grouped = consts.tile([P, B * PACK], BF16, align_bytes=64)
+        nc.vector.tensor_copy(
+            out=x_grouped[:].bitcast(F32).rearrange("p (b u) -> p b u", u=2),
+            in_=xT_ps[:].rearrange("p u b -> p b u"),
+        )
+        x_codes = consts.tile([P, B], U32, align_bytes=64)
+        x_scales = consts.tile([P, B], U8, align_bytes=64)
+        nc.vector.quantize_mx(out=x_codes[:].bitcast(FP8X4), scales=x_scales[:], in_=x_grouped[:])
+
+        b1_rows_f32 = consts.tile([P, P], F32)
+        nc.vector.tensor_copy(out=b1_rows_f32[:], in_=b1_rows[:])
+        b1T_ps = psum_setup.tile([P, P], F32)
+        nc.tensor.transpose(b1T_ps[:], b1_rows_f32[:], ident[:])
+        b1T = consts.tile([P, E * PACK], F32)
+        nc.vector.tensor_copy(out=b1T[:], in_=b1T_ps[:, 0 : E * PACK])
+
+        b2_ps = psum_setup.tile([P, E * L], F32)
+        nc.tensor.matmul(b2_ps[:], lhsT=ones[:], rhs=b2_row[:], start=True, stop=True)
+
+        abs_pre = consts.tile([B, E], F32)
+        nc.scalar.activation(out=abs_pre[:], in_=pre[:], func=ACT.Abs)
+        exp_pre = consts.tile([B, E], F32)
+        nc.scalar.activation(out=exp_pre[:], in_=abs_pre[:], func=ACT.Exp, scale=-1.0)
+        log_pre = consts.tile([B, E], F32)
+        nc.scalar.activation(out=log_pre[:], in_=exp_pre[:], func=ACT.Ln, bias=one_col[:, 0:1])
+        relu_pre = consts.tile([B, E], F32)
+        nc.vector.tensor_scalar(
+            out=relu_pre[:], in0=pre[:], scalar1=0.0, scalar2=NOISE_EPS, op0=ALU.max, op1=ALU.add
+        )
+        sd = consts.tile([B, E], F32)
+        nc.vector.tensor_tensor(out=sd[:], in0=log_pre[:], in1=relu_pre[:], op=ALU.add)
+        scaled_noise = consts.tile([B, E], F32)
+        nc.vector.tensor_tensor(out=scaled_noise[:], in0=sd[:], in1=eps_noise[:], op=ALU.mult)
+        logits = consts.tile([B, E], F32)
+        nc.vector.tensor_tensor(out=logits[:], in0=scaled_noise[:], in1=clean[:], op=ALU.add)
+        row_max = consts.tile([B, 1], F32)
+        nc.vector.reduce_max(out=row_max[:], in_=logits[:], axis=AX.X)
+        neg_max = consts.tile([B, 1], F32)
+        nc.vector.tensor_scalar_mul(neg_max[:], row_max[:], -1.0)
+        ex = consts.tile([B, E], F32)
+        ex_sum = consts.tile([B, 1], F32)
+        nc.scalar.activation(
+            out=ex[:], in_=logits[:], func=ACT.Exp, bias=neg_max[:, 0:1], accum_out=ex_sum[:, 0:1]
+        )
+        threshold = consts.tile([B, 1], F32)
+        nc.vector.tensor_scalar_mul(threshold[:], ex_sum[:], 1.0 / E - MEAN_EPS)
+        kept = consts.tile([B, E], F32)
+        nc.vector.scalar_tensor_tensor(
+            out=kept[:], in0=ex[:], scalar=threshold[:, 0:1], in1=ex[:], op0=ALU.is_ge, op1=ALU.mult
+        )
+        kept_sum = consts.tile([B, 1], F32)
+        nc.vector.reduce_sum(out=kept_sum[:], in_=kept[:], axis=AX.X)
+        inv_sum = consts.tile([B, 1], F32)
+        nc.vector.reciprocal(out=inv_sum[:], in_=kept_sum[:])
+        gates = consts.tile([B, E], F32)
+        nc.vector.tensor_scalar_mul(gates[:], kept[:], inv_sum[:, 0:1])
+        gated_b2 = consts.tile([B, E, L], F32)
+        nc.vector.tensor_tensor(
+            out=gated_b2[:],
+            in0=b2_ps[:].rearrange("p (e l) -> p e l", l=L),
+            in1=gates[:].unsqueeze(2).to_broadcast([B, E, L]),
+            op=ALU.mult,
+        )
+
+        w1_codes = consts.tile([P, E, H], U32, align_bytes=64)
+        w1_scales = consts.tile([P, E, H], U8, align_bytes=64)
+        w2_codes = consts.tile([P, E // E_HALF, E_HALF * L], U32, align_bytes=64)
+        w2_scales = consts.tile([P, E // E_HALF, E_HALF * L], U8, align_bytes=64)
+        result = consts.tile([B, E, L], F32)
+
+        for e in range(E):
+            a, c = divmod(e, E_HALF)
+            if c == 0:
+                w2_grouped = stage.tile([P, E_HALF, L, PACK], BF16, align_bytes=64)
+                nc.vector.tensor_copy(
+                    out=w2_grouped[:], in_=w2_raw[a][:].rearrange("p e t l -> p e l t")
+                )
+                nc.vector.quantize_mx(
+                    out=w2_codes[:, a, :].bitcast(FP8X4),
+                    scales=w2_scales[:, a, :],
+                    in_=w2_grouped[:].rearrange("p e l t -> p (e l t)"),
+                )
+
+            w1_grouped = stage.tile([P, H, PACK], BF16, align_bytes=64)
+            regroup(nc.vector.tensor_copy, w1_grouped[:, 0:VECTOR_COLS, :], w1_raw[e][:, :, 0:VECTOR_COLS])
+            regroup(nc.scalar.copy, w1_grouped[:, VECTOR_COLS:H, :], w1_raw[e][:, :, VECTOR_COLS:H])
+            nc.vector.quantize_mx(
+                out=w1_codes[:, e, :].bitcast(FP8X4),
+                scales=w1_scales[:, e, :],
+                in_=w1_grouped[:].rearrange("p h j -> p (h j)"),
+            )
+
+            hT_ps = psum_h.tile([P, PACK, B], F32)
+            for t in range(PACK):
+                cols = slice(t * P, (t + 1) * P)
+                nc.tensor.matmul_mx(
+                    out=hT_ps[:, t, :],
+                    lhsT=w1_codes[:, e, cols].bitcast(FP8X4),
+                    lhsT_scale=w1_scales[:, e, cols],
+                    rhs=x_codes[:].bitcast(FP8X4),
+                    rhs_scale=x_scales[:],
+                    start=True,
+                    stop=True,
+                )
+            h_planes = stage.tile([P, PACK, B], BF16)
+            for t in range(PACK):
+                nc.scalar.activation(
+                    out=h_planes[:, t, :],
+                    in_=hT_ps[:, t, :],
+                    func=ACT.Tanh,
+                    bias=b1T[:, e * PACK + t : e * PACK + t + 1],
+                )
+            h_grouped = stage.tile([P, B, PACK], BF16, align_bytes=64)
+            regroup(nc.vector.tensor_copy, h_grouped[:], h_planes[:])
+            h_codes = stage.tile([P, B], U32, align_bytes=64)
+            h_scales = stage.tile([P, B], U8, align_bytes=64)
+            nc.vector.quantize_mx(
+                out=h_codes[:].bitcast(FP8X4),
+                scales=h_scales[:],
+                in_=h_grouped[:].rearrange("p b t -> p (b t)"),
+            )
+
+            y_ps = psum_y.tile([B, E_HALF * L], F32)
+            nc.tensor.matmul_mx(
+                out=y_ps[:],
+                lhsT=h_codes[:].bitcast(FP8X4),
+                lhsT_scale=h_scales[:],
+                rhs=w2_codes[:, a, :].bitcast(FP8X4),
+                rhs_scale=w2_scales[:, a, :],
+                start=True,
+                stop=True,
+            )
+            nc.vector.scalar_tensor_tensor(
+                out=result[:, e, :],
+                in0=y_ps[:, c * L : (c + 1) * L],
+                scalar=gates[:, e : e + 1],
+                in1=gated_b2[:, e, :],
+                op0=ALU.mult,
+                op1=ALU.add,
+            )
+
+        nc.sync.dma_start(out=out, in_=result[:])

@@ -20,7 +20,12 @@ P = 128
 PACK = 4
 E_HALF = 4
 RUN = 4
-VECTOR_COLS = 256
+VECTOR_COLS = 288
+
+REGROUP_AHEAD = 3
+PRODUCT_AHEAD = 2
+SECOND_BEHIND = 1
+FINISH_BEHIND = 2
 
 FLOPS = 2 * B * D * H * E + 2 * B * H * L * E
 
@@ -35,11 +40,11 @@ def regroup(copy, dst, src):
 def tile_mblfe_pa_s_kernel(tc, x, noise, clean_logits, noise_pre, W1, b1, W2, b2, out):
     nc = tc.nc
     with ExitStack() as ctx:
+        ctx.enter_context(tc.manual_schedule())
         consts = ctx.enter_context(tc.tile_pool(name="consts", bufs=1))
-        w1_in = ctx.enter_context(tc.tile_pool(name="w1_in", bufs=E))
-        stage = ctx.enter_context(tc.tile_pool(name="stage", bufs=3))
+        stage = ctx.enter_context(tc.tile_pool(name="stage", bufs=2))
         psum_setup = ctx.enter_context(tc.psum_pool(name="psum_setup", bufs=1))
-        psum_h = ctx.enter_context(tc.psum_pool(name="psum_h", bufs=3))
+        psum_h = ctx.enter_context(tc.psum_pool(name="psum_h", bufs=PRODUCT_AHEAD + 1))
         psum_y = ctx.enter_context(tc.psum_pool(name="psum_y", bufs=2))
 
         b1_rows = consts.tile([P, P], BF16)
@@ -51,56 +56,143 @@ def tile_mblfe_pa_s_kernel(tc, x, noise, clean_logits, noise_pre, W1, b1, W2, b2
         one_col = consts.tile([P, 1], F32)
         nc.vector.memset(one_col[:], 1.0)
 
-        pre = consts.tile([B, E], BF16)
-        nc.scalar.dma_start(out=pre[:], in_=noise_pre)
-        eps_noise = consts.tile([B, E], BF16)
-        nc.scalar.dma_start(out=eps_noise[:], in_=noise)
-        clean = consts.tile([B, E], BF16)
-        nc.scalar.dma_start(out=clean[:], in_=clean_logits)
-        nc.scalar.dma_start(out=b1_rows[0 : E * PACK, :], in_=b1.rearrange("e (t p) -> (e t) p", p=P))
-        nc.scalar.dma_start(out=b2_row[0:1, :], in_=b2.rearrange("(o e) l -> o (e l)", o=1))
+        w1_raw = {}
+        w2_raw = {}
 
+        def load_w1(e):
+            w1_raw[e] = consts.tile([P, PACK, H], BF16, name="w1_raw%d" % e)
+            nc.sync.dma_start(out=w1_raw[e][:], in_=W1[e].rearrange("(p j) h -> p j h", j=PACK))
+
+        def load_w2(a):
+            w2_raw[a] = consts.tile([P, E_HALF, PACK, L], BF16, name="w2_raw%d" % a)
+            four = slice(a * E_HALF, (a + 1) * E_HALF)
+            nc.sync.dma_start(out=w2_raw[a][:], in_=W2[four].rearrange("e (t p) l -> p e t l", p=P))
+
+        pre = consts.tile([B, E], BF16)
+        nc.sync.dma_start(out=pre[:], in_=noise_pre)
+        load_w1(0)
+        eps_noise = consts.tile([B, E], BF16)
+        nc.sync.dma_start(out=eps_noise[:], in_=noise)
+        clean = consts.tile([B, E], BF16)
+        nc.sync.dma_start(out=clean[:], in_=clean_logits)
+        nc.sync.dma_start(out=b1_rows[0 : E * PACK, :], in_=b1.rearrange("e (t p) -> (e t) p", p=P))
         x_rows = consts.tile([B, D], BF16)
         nc.sync.dma_start(out=x_rows[:], in_=x)
-        w1_raw = []
-        w2_raw = []
-        for e in range(E):
-            raw = w1_in.tile([P, PACK, H], BF16)
-            nc.sync.dma_start(out=raw[:], in_=W1[e].rearrange("(p j) h -> p j h", j=PACK))
-            w1_raw.append(raw)
-            if e % E_HALF == 1:
-                a = e // E_HALF
-                raw2 = consts.tile([P, E_HALF, PACK, L], BF16, name="w2_raw%d" % a)
-                nc.sync.dma_start(
-                    out=raw2[:],
-                    in_=W2[a * E_HALF : (a + 1) * E_HALF].rearrange("e (t p) l -> p e t l", p=P),
-                )
-                w2_raw.append(raw2)
+        load_w1(1)
+        nc.sync.dma_start(out=b2_row[0:1, :], in_=b2.rearrange("(o e) l -> o (e l)", o=1))
+        load_w1(2)
+        load_w2(0)
+        load_w1(3)
+        load_w1(4)
+        load_w1(5)
+        load_w2(1)
+        load_w1(6)
+        load_w1(7)
 
         ident = consts.tile([P, P], F32)
         make_identity(nc, ident[:])
-        x_words = x_rows[:].bitcast(F32).rearrange("b (p u) -> b u p", u=2)
-        xT_ps = psum_setup.tile([P, 2, B], F32)
-        for u in range(2):
-            nc.tensor.transpose(xT_ps[:, u, :], x_words[:, u, :], ident[:])
-        x_grouped = consts.tile([P, B * PACK], BF16, align_bytes=64)
-        nc.vector.tensor_copy(
-            out=x_grouped[:].bitcast(F32).rearrange("p (b u) -> p b u", u=2),
-            in_=xT_ps[:].rearrange("p u b -> p b u"),
-        )
+
         x_codes = consts.tile([P, B], U32, align_bytes=64)
         x_scales = consts.tile([P, B], U8, align_bytes=64)
-        nc.vector.quantize_mx(out=x_codes[:].bitcast(FP8X4), scales=x_scales[:], in_=x_grouped[:])
-
-        b1_rows_f32 = consts.tile([P, P], F32)
-        nc.vector.tensor_copy(out=b1_rows_f32[:], in_=b1_rows[:])
-        b1T_ps = psum_setup.tile([P, P], F32)
-        nc.tensor.transpose(b1T_ps[:], b1_rows_f32[:], ident[:])
+        w2_codes = consts.tile([P, E // E_HALF, E_HALF * L], U32, align_bytes=64)
+        w2_scales = consts.tile([P, E // E_HALF, E_HALF * L], U8, align_bytes=64)
         b1T = consts.tile([P, E * PACK], F32)
-        nc.vector.tensor_copy(out=b1T[:], in_=b1T_ps[:, 0 : E * PACK])
+        gates = consts.tile([B, E], F32)
+        gated_b2 = consts.tile([B, E, L], F32)
+        result = consts.tile([B, E, L], F32)
+        w1_grouped = {}
+        w1_codes = {}
+        w1_scales = {}
+        w2_grouped = {}
+        hT_ps = {}
+        h_planes = {}
+        h_grouped = {}
+        h_codes = {}
+        h_scales = {}
+        y_ps = {}
 
-        b2_ps = psum_setup.tile([P, E * L], F32)
-        nc.tensor.matmul(b2_ps[:], lhsT=ones[:], rhs=b2_row[:], start=True, stop=True)
+        def regroup_w1_on_vector(e):
+            w1_grouped[e] = stage.tile([P, H, PACK], BF16, align_bytes=64, name="w1_grouped")
+            regroup(nc.vector.tensor_copy, w1_grouped[e][:, 0:VECTOR_COLS, :], w1_raw[e][:, :, 0:VECTOR_COLS])
+
+        def regroup_w1_on_scalar(e):
+            regroup(nc.scalar.copy, w1_grouped[e][:, VECTOR_COLS:H, :], w1_raw[e][:, :, VECTOR_COLS:H])
+
+        def first_product(e):
+            w1_codes[e] = stage.tile([P, H], U32, align_bytes=64, name="w1_codes")
+            w1_scales[e] = stage.tile([P, H], U8, align_bytes=64, name="w1_scales")
+            nc.vector.quantize_mx(
+                out=w1_codes[e][:].bitcast(FP8X4),
+                scales=w1_scales[e][:],
+                in_=w1_grouped[e][:].rearrange("p h j -> p (h j)"),
+            )
+            hT_ps[e] = psum_h.tile([P, PACK, B], F32, name="hT_ps")
+            for t in range(PACK):
+                cols = slice(t * P, (t + 1) * P)
+                nc.tensor.matmul_mx(
+                    out=hT_ps[e][:, t, :],
+                    lhsT=w1_codes[e][:, cols].bitcast(FP8X4),
+                    lhsT_scale=w1_scales[e][:, cols],
+                    rhs=x_codes[:].bitcast(FP8X4),
+                    rhs_scale=x_scales[:],
+                    start=True,
+                    stop=True,
+                )
+
+        def tanh(e):
+            h_planes[e] = stage.tile([P, PACK, B], BF16, name="h_planes")
+            for t in range(PACK):
+                nc.scalar.activation(
+                    out=h_planes[e][:, t, :],
+                    in_=hT_ps[e][:, t, :],
+                    func=ACT.Tanh,
+                    bias=b1T[:, e * PACK + t : e * PACK + t + 1],
+                )
+
+        def regroup_h(e):
+            h_grouped[e] = stage.tile([P, B, PACK], BF16, align_bytes=64, name="h_grouped")
+            regroup(nc.vector.tensor_copy, h_grouped[e][:], h_planes[e][:])
+
+        def regroup_w2(a):
+            w2_grouped[a] = stage.tile([P, E_HALF, L, PACK], BF16, align_bytes=64, name="w2_grouped")
+            nc.vector.tensor_copy(out=w2_grouped[a][:], in_=w2_raw[a][:].rearrange("p e t l -> p e l t"))
+
+        def quantise_w2(a):
+            nc.vector.quantize_mx(
+                out=w2_codes[:, a, :].bitcast(FP8X4),
+                scales=w2_scales[:, a, :],
+                in_=w2_grouped[a][:].rearrange("p e l t -> p (e l t)"),
+            )
+
+        def second_product(e):
+            h_codes[e] = stage.tile([P, B], U32, align_bytes=64, name="h_codes")
+            h_scales[e] = stage.tile([P, B], U8, align_bytes=64, name="h_scales")
+            nc.vector.quantize_mx(
+                out=h_codes[e][:].bitcast(FP8X4),
+                scales=h_scales[e][:],
+                in_=h_grouped[e][:].rearrange("p b t -> p (b t)"),
+            )
+            a = e // E_HALF
+            y_ps[e] = psum_y.tile([B, E_HALF, L], F32, name="y_ps")
+            nc.tensor.matmul_mx(
+                out=y_ps[e][:].rearrange("b c l -> b (c l)"),
+                lhsT=h_codes[e][:].bitcast(FP8X4),
+                lhsT_scale=h_scales[e][:],
+                rhs=w2_codes[:, a, :].bitcast(FP8X4),
+                rhs_scale=w2_scales[:, a, :],
+                start=True,
+                stop=True,
+            )
+
+        def finish(e):
+            nc.vector.scalar_tensor_tensor(
+                out=result[:, e, :],
+                in0=y_ps[e][:, e % E_HALF, :],
+                scalar=gates[:, e : e + 1],
+                in1=gated_b2[:, e, :],
+                op0=ALU.mult,
+                op1=ALU.add,
+            )
 
         abs_pre = consts.tile([B, E], F32)
         nc.scalar.activation(out=abs_pre[:], in_=pre[:], func=ACT.Abs)
@@ -112,6 +204,29 @@ def tile_mblfe_pa_s_kernel(tc, x, noise, clean_logits, noise_pre, W1, b1, W2, b2
         nc.vector.tensor_scalar(
             out=relu_pre[:], in0=pre[:], scalar1=0.0, scalar2=NOISE_EPS, op0=ALU.max, op1=ALU.add
         )
+
+        regroup_w1_on_vector(0)
+        regroup_w1_on_scalar(0)
+
+        x_words = x_rows[:].bitcast(F32).rearrange("b (p u) -> b u p", u=2)
+        xT_ps = psum_setup.tile([P, 2, B], F32)
+        for u in range(2):
+            nc.tensor.transpose(xT_ps[:, u, :], x_words[:, u, :], ident[:])
+        b1_rows_f32 = consts.tile([P, P], F32)
+        nc.vector.tensor_copy(out=b1_rows_f32[:], in_=b1_rows[:])
+        b1T_ps = psum_setup.tile([P, P], F32)
+        nc.tensor.transpose(b1T_ps[:], b1_rows_f32[:], ident[:])
+        b2_ps = psum_setup.tile([P, E, L], F32)
+        nc.tensor.matmul(
+            b2_ps[:].rearrange("p e l -> p (e l)"), lhsT=ones[:], rhs=b2_row[:], start=True, stop=True
+        )
+
+        x_grouped = consts.tile([P, B * PACK], BF16, align_bytes=64)
+        nc.vector.tensor_copy(
+            out=x_grouped[:].bitcast(F32).rearrange("p (b u) -> p b u", u=2),
+            in_=xT_ps[:].rearrange("p u b -> p b u"),
+        )
+
         sd = consts.tile([B, E], F32)
         nc.vector.tensor_tensor(out=sd[:], in0=log_pre[:], in1=relu_pre[:], op=ALU.add)
         scaled_noise = consts.tile([B, E], F32)
@@ -122,106 +237,59 @@ def tile_mblfe_pa_s_kernel(tc, x, noise, clean_logits, noise_pre, W1, b1, W2, b2
         nc.vector.reduce_max(out=row_max[:], in_=logits[:], axis=AX.X)
         neg_max = consts.tile([B, 1], F32)
         nc.vector.tensor_scalar_mul(neg_max[:], row_max[:], -1.0)
+
+        nc.vector.tensor_copy(out=b1T[:], in_=b1T_ps[:, 0 : E * PACK])
+        nc.vector.quantize_mx(out=x_codes[:].bitcast(FP8X4), scales=x_scales[:], in_=x_grouped[:])
+
         ex = consts.tile([B, E], F32)
         ex_sum = consts.tile([B, 1], F32)
-        nc.scalar.activation(
-            out=ex[:], in_=logits[:], func=ACT.Exp, bias=neg_max[:, 0:1], accum_out=ex_sum[:, 0:1]
-        )
-        threshold = consts.tile([B, 1], F32)
-        nc.vector.tensor_scalar_mul(threshold[:], ex_sum[:], 1.0 / E - MEAN_EPS)
-        kept = consts.tile([B, E], F32)
-        nc.vector.scalar_tensor_tensor(
-            out=kept[:], in0=ex[:], scalar=threshold[:, 0:1], in1=ex[:], op0=ALU.is_ge, op1=ALU.mult
-        )
-        kept_sum = consts.tile([B, 1], F32)
-        nc.vector.reduce_sum(out=kept_sum[:], in_=kept[:], axis=AX.X)
-        inv_sum = consts.tile([B, 1], F32)
-        nc.vector.reciprocal(out=inv_sum[:], in_=kept_sum[:])
-        gates = consts.tile([B, E], F32)
-        nc.vector.tensor_scalar_mul(gates[:], kept[:], inv_sum[:, 0:1])
-        gated_b2 = consts.tile([B, E, L], F32)
-        nc.vector.tensor_tensor(
-            out=gated_b2[:],
-            in0=b2_ps[:].rearrange("p (e l) -> p e l", l=L),
-            in1=gates[:].unsqueeze(2).to_broadcast([B, E, L]),
-            op=ALU.mult,
-        )
 
-        w1_codes = consts.tile([P, E, H], U32, align_bytes=64)
-        w1_scales = consts.tile([P, E, H], U8, align_bytes=64)
-        w2_codes = consts.tile([P, E // E_HALF, E_HALF * L], U32, align_bytes=64)
-        w2_scales = consts.tile([P, E // E_HALF, E_HALF * L], U8, align_bytes=64)
-        result = consts.tile([B, E, L], F32)
-
-        for e in range(E):
-            a, c = divmod(e, E_HALF)
-            if c == 0:
-                w2_grouped = stage.tile([P, E_HALF, L, PACK], BF16, align_bytes=64)
-                nc.vector.tensor_copy(
-                    out=w2_grouped[:], in_=w2_raw[a][:].rearrange("p e t l -> p e l t")
-                )
-                nc.vector.quantize_mx(
-                    out=w2_codes[:, a, :].bitcast(FP8X4),
-                    scales=w2_scales[:, a, :],
-                    in_=w2_grouped[:].rearrange("p e l t -> p (e l t)"),
-                )
-
-            w1_grouped = stage.tile([P, H, PACK], BF16, align_bytes=64)
-            regroup(nc.vector.tensor_copy, w1_grouped[:, 0:VECTOR_COLS, :], w1_raw[e][:, :, 0:VECTOR_COLS])
-            regroup(nc.scalar.copy, w1_grouped[:, VECTOR_COLS:H, :], w1_raw[e][:, :, VECTOR_COLS:H])
-            nc.vector.quantize_mx(
-                out=w1_codes[:, e, :].bitcast(FP8X4),
-                scales=w1_scales[:, e, :],
-                in_=w1_grouped[:].rearrange("p h j -> p (h j)"),
+        def softmax_exponentials():
+            nc.scalar.activation(
+                out=ex[:], in_=logits[:], func=ACT.Exp, bias=neg_max[:, 0:1], accum_out=ex_sum[:, 0:1]
             )
 
-            hT_ps = psum_h.tile([P, PACK, B], F32)
-            for t in range(PACK):
-                cols = slice(t * P, (t + 1) * P)
-                nc.tensor.matmul_mx(
-                    out=hT_ps[:, t, :],
-                    lhsT=w1_codes[:, e, cols].bitcast(FP8X4),
-                    lhsT_scale=w1_scales[:, e, cols],
-                    rhs=x_codes[:].bitcast(FP8X4),
-                    rhs_scale=x_scales[:],
-                    start=True,
-                    stop=True,
-                )
-            h_planes = stage.tile([P, PACK, B], BF16)
-            for t in range(PACK):
-                nc.scalar.activation(
-                    out=h_planes[:, t, :],
-                    in_=hT_ps[:, t, :],
-                    func=ACT.Tanh,
-                    bias=b1T[:, e * PACK + t : e * PACK + t + 1],
-                )
-            h_grouped = stage.tile([P, B, PACK], BF16, align_bytes=64)
-            regroup(nc.vector.tensor_copy, h_grouped[:], h_planes[:])
-            h_codes = stage.tile([P, B], U32, align_bytes=64)
-            h_scales = stage.tile([P, B], U8, align_bytes=64)
-            nc.vector.quantize_mx(
-                out=h_codes[:].bitcast(FP8X4),
-                scales=h_scales[:],
-                in_=h_grouped[:].rearrange("p b t -> p (b t)"),
-            )
-
-            y_ps = psum_y.tile([B, E_HALF * L], F32)
-            nc.tensor.matmul_mx(
-                out=y_ps[:],
-                lhsT=h_codes[:].bitcast(FP8X4),
-                lhsT_scale=h_scales[:],
-                rhs=w2_codes[:, a, :].bitcast(FP8X4),
-                rhs_scale=w2_scales[:, a, :],
-                start=True,
-                stop=True,
-            )
+        def gates_from_exponentials():
+            threshold = consts.tile([B, 1], F32)
+            nc.vector.tensor_scalar_mul(threshold[:], ex_sum[:], 1.0 / E - MEAN_EPS)
+            kept = consts.tile([B, E], F32)
             nc.vector.scalar_tensor_tensor(
-                out=result[:, e, :],
-                in0=y_ps[:, c * L : (c + 1) * L],
-                scalar=gates[:, e : e + 1],
-                in1=gated_b2[:, e, :],
-                op0=ALU.mult,
-                op1=ALU.add,
+                out=kept[:], in0=ex[:], scalar=threshold[:, 0:1], in1=ex[:], op0=ALU.is_ge, op1=ALU.mult
             )
+            kept_sum = consts.tile([B, 1], F32)
+            nc.vector.reduce_sum(out=kept_sum[:], in_=kept[:], axis=AX.X)
+            inv_sum = consts.tile([B, 1], F32)
+            nc.vector.reciprocal(out=inv_sum[:], in_=kept_sum[:])
+            nc.vector.tensor_scalar_mul(gates[:], kept[:], inv_sum[:, 0:1])
+            nc.vector.tensor_tensor(
+                out=gated_b2[:], in0=b2_ps[:], in1=gates[:].unsqueeze(2).to_broadcast([B, E, L]), op=ALU.mult
+            )
+
+        def live(e):
+            return 0 <= e < E
+
+        for s in range(1 - REGROUP_AHEAD, E + FINISH_BEHIND):
+            if live(s + REGROUP_AHEAD):
+                regroup_w1_on_vector(s + REGROUP_AHEAD)
+            if live(s - SECOND_BEHIND):
+                regroup_h(s - SECOND_BEHIND)
+            if live(s) and s % E_HALF == 0:
+                regroup_w2(s // E_HALF)
+            if live(s + PRODUCT_AHEAD):
+                first_product(s + PRODUCT_AHEAD)
+            if live(s) and s % E_HALF == 0:
+                quantise_w2(s // E_HALF)
+            if live(s - SECOND_BEHIND):
+                second_product(s - SECOND_BEHIND)
+            if s == FINISH_BEHIND:
+                gates_from_exponentials()
+            if live(s - FINISH_BEHIND):
+                finish(s - FINISH_BEHIND)
+            if s == 0:
+                softmax_exponentials()
+            if live(s):
+                tanh(s)
+            if live(s + REGROUP_AHEAD):
+                regroup_w1_on_scalar(s + REGROUP_AHEAD)
 
         nc.sync.dma_start(out=out, in_=result[:])

@@ -18,14 +18,14 @@ MEAN_EPS = 1e-8
 
 P = 128
 PACK = 4
-E_HALF = 4
+N_MIN = 128
 RUN = 4
 VECTOR_COLS = 288
+PSUM_BANKS = 8
+Y_BANKS = 2
 
-REGROUP_AHEAD = 3
-PRODUCT_AHEAD = 2
 SECOND_BEHIND = 1
-FINISH_BEHIND = 2
+FINISH_BEHIND = 3
 
 FLOPS = 2 * B * D * H * E + 2 * B * H * L * E
 
@@ -42,10 +42,8 @@ def tile_mblfe_pa_s_kernel(tc, x, noise, clean_logits, noise_pre, W1, b1, W2, b2
     with ExitStack() as ctx:
         ctx.enter_context(tc.manual_schedule())
         consts = ctx.enter_context(tc.tile_pool(name="consts", bufs=1))
-        stage = ctx.enter_context(tc.tile_pool(name="stage", bufs=2))
-        psum_setup = ctx.enter_context(tc.psum_pool(name="psum_setup", bufs=1))
-        psum_h = ctx.enter_context(tc.psum_pool(name="psum_h", bufs=PRODUCT_AHEAD + 1))
-        psum_y = ctx.enter_context(tc.psum_pool(name="psum_y", bufs=2))
+        per_expert = ctx.enter_context(tc.tile_pool(name="per_expert", bufs=E))
+        stage = ctx.enter_context(tc.tile_pool(name="stage", bufs=3))
 
         b1_rows = consts.tile([P, P], BF16)
         nc.vector.memset(b1_rows[:], 0.0)
@@ -56,143 +54,30 @@ def tile_mblfe_pa_s_kernel(tc, x, noise, clean_logits, noise_pre, W1, b1, W2, b2
         one_col = consts.tile([P, 1], F32)
         nc.vector.memset(one_col[:], 1.0)
 
-        w1_raw = {}
-        w2_raw = {}
-
-        def load_w1(e):
-            w1_raw[e] = consts.tile([P, PACK, H], BF16, name="w1_raw%d" % e)
-            nc.sync.dma_start(out=w1_raw[e][:], in_=W1[e].rearrange("(p j) h -> p j h", j=PACK))
-
-        def load_w2(a):
-            w2_raw[a] = consts.tile([P, E_HALF, PACK, L], BF16, name="w2_raw%d" % a)
-            four = slice(a * E_HALF, (a + 1) * E_HALF)
-            nc.sync.dma_start(out=w2_raw[a][:], in_=W2[four].rearrange("e (t p) l -> p e t l", p=P))
-
         pre = consts.tile([B, E], BF16)
         nc.sync.dma_start(out=pre[:], in_=noise_pre)
+        x_rows = consts.tile([B, D], BF16)
+        nc.sync.dma_start(out=x_rows[:], in_=x)
+        nc.sync.dma_start(out=b1_rows[0 : E * PACK, :], in_=b1.rearrange("e (t p) -> (e t) p", p=P))
+        nc.sync.dma_start(out=b2_row[0:1, :], in_=b2.rearrange("(o e) l -> o (e l)", o=1))
+        w1_raw = {}
+
+        def load_w1(e):
+            w1_raw[e] = per_expert.tile([P, PACK, H], BF16, name="w1_raw")
+            nc.sync.dma_start(out=w1_raw[e][:], in_=W1[e].rearrange("(p j) h -> p j h", j=PACK))
+
         load_w1(0)
         eps_noise = consts.tile([B, E], BF16)
         nc.sync.dma_start(out=eps_noise[:], in_=noise)
         clean = consts.tile([B, E], BF16)
         nc.sync.dma_start(out=clean[:], in_=clean_logits)
-        nc.sync.dma_start(out=b1_rows[0 : E * PACK, :], in_=b1.rearrange("e (t p) -> (e t) p", p=P))
-        x_rows = consts.tile([B, D], BF16)
-        nc.sync.dma_start(out=x_rows[:], in_=x)
-        load_w1(1)
-        nc.sync.dma_start(out=b2_row[0:1, :], in_=b2.rearrange("(o e) l -> o (e l)", o=1))
-        load_w1(2)
-        load_w2(0)
-        load_w1(3)
-        load_w1(4)
-        load_w1(5)
-        load_w2(1)
-        load_w1(6)
-        load_w1(7)
+        for e in range(1, E):
+            load_w1(e)
+        w2_raw = consts.tile([P, E, PACK, L], BF16)
+        nc.sync.dma_start(out=w2_raw[:], in_=W2.rearrange("e (t p) l -> p e t l", p=P))
 
         ident = consts.tile([P, P], F32)
         make_identity(nc, ident[:])
-
-        x_codes = consts.tile([P, B], U32, align_bytes=64)
-        x_scales = consts.tile([P, B], U8, align_bytes=64)
-        w2_codes = consts.tile([P, E // E_HALF, E_HALF * L], U32, align_bytes=64)
-        w2_scales = consts.tile([P, E // E_HALF, E_HALF * L], U8, align_bytes=64)
-        b1T = consts.tile([P, E * PACK], F32)
-        gates = consts.tile([B, E], F32)
-        gated_b2 = consts.tile([B, E, L], F32)
-        result = consts.tile([B, E, L], F32)
-        w1_grouped = {}
-        w1_codes = {}
-        w1_scales = {}
-        w2_grouped = {}
-        hT_ps = {}
-        h_planes = {}
-        h_grouped = {}
-        h_codes = {}
-        h_scales = {}
-        y_ps = {}
-
-        def regroup_w1_on_vector(e):
-            w1_grouped[e] = stage.tile([P, H, PACK], BF16, align_bytes=64, name="w1_grouped")
-            regroup(nc.vector.tensor_copy, w1_grouped[e][:, 0:VECTOR_COLS, :], w1_raw[e][:, :, 0:VECTOR_COLS])
-
-        def regroup_w1_on_scalar(e):
-            regroup(nc.scalar.copy, w1_grouped[e][:, VECTOR_COLS:H, :], w1_raw[e][:, :, VECTOR_COLS:H])
-
-        def first_product(e):
-            w1_codes[e] = stage.tile([P, H], U32, align_bytes=64, name="w1_codes")
-            w1_scales[e] = stage.tile([P, H], U8, align_bytes=64, name="w1_scales")
-            nc.vector.quantize_mx(
-                out=w1_codes[e][:].bitcast(FP8X4),
-                scales=w1_scales[e][:],
-                in_=w1_grouped[e][:].rearrange("p h j -> p (h j)"),
-            )
-            hT_ps[e] = psum_h.tile([P, PACK, B], F32, name="hT_ps")
-            for t in range(PACK):
-                cols = slice(t * P, (t + 1) * P)
-                nc.tensor.matmul_mx(
-                    out=hT_ps[e][:, t, :],
-                    lhsT=w1_codes[e][:, cols].bitcast(FP8X4),
-                    lhsT_scale=w1_scales[e][:, cols],
-                    rhs=x_codes[:].bitcast(FP8X4),
-                    rhs_scale=x_scales[:],
-                    start=True,
-                    stop=True,
-                )
-
-        def tanh(e):
-            h_planes[e] = stage.tile([P, PACK, B], BF16, name="h_planes")
-            for t in range(PACK):
-                nc.scalar.activation(
-                    out=h_planes[e][:, t, :],
-                    in_=hT_ps[e][:, t, :],
-                    func=ACT.Tanh,
-                    bias=b1T[:, e * PACK + t : e * PACK + t + 1],
-                )
-
-        def regroup_h(e):
-            h_grouped[e] = stage.tile([P, B, PACK], BF16, align_bytes=64, name="h_grouped")
-            regroup(nc.vector.tensor_copy, h_grouped[e][:], h_planes[e][:])
-
-        def regroup_w2(a):
-            w2_grouped[a] = stage.tile([P, E_HALF, L, PACK], BF16, align_bytes=64, name="w2_grouped")
-            nc.vector.tensor_copy(out=w2_grouped[a][:], in_=w2_raw[a][:].rearrange("p e t l -> p e l t"))
-
-        def quantise_w2(a):
-            nc.vector.quantize_mx(
-                out=w2_codes[:, a, :].bitcast(FP8X4),
-                scales=w2_scales[:, a, :],
-                in_=w2_grouped[a][:].rearrange("p e l t -> p (e l t)"),
-            )
-
-        def second_product(e):
-            h_codes[e] = stage.tile([P, B], U32, align_bytes=64, name="h_codes")
-            h_scales[e] = stage.tile([P, B], U8, align_bytes=64, name="h_scales")
-            nc.vector.quantize_mx(
-                out=h_codes[e][:].bitcast(FP8X4),
-                scales=h_scales[e][:],
-                in_=h_grouped[e][:].rearrange("p b t -> p (b t)"),
-            )
-            a = e // E_HALF
-            y_ps[e] = psum_y.tile([B, E_HALF, L], F32, name="y_ps")
-            nc.tensor.matmul_mx(
-                out=y_ps[e][:].rearrange("b c l -> b (c l)"),
-                lhsT=h_codes[e][:].bitcast(FP8X4),
-                lhsT_scale=h_scales[e][:],
-                rhs=w2_codes[:, a, :].bitcast(FP8X4),
-                rhs_scale=w2_scales[:, a, :],
-                start=True,
-                stop=True,
-            )
-
-        def finish(e):
-            nc.vector.scalar_tensor_tensor(
-                out=result[:, e, :],
-                in0=y_ps[e][:, e % E_HALF, :],
-                scalar=gates[:, e : e + 1],
-                in1=gated_b2[:, e, :],
-                op0=ALU.mult,
-                op1=ALU.add,
-            )
 
         abs_pre = consts.tile([B, E], F32)
         nc.scalar.activation(out=abs_pre[:], in_=pre[:], func=ACT.Abs)
@@ -205,27 +90,65 @@ def tile_mblfe_pa_s_kernel(tc, x, noise, clean_logits, noise_pre, W1, b1, W2, b2
             out=relu_pre[:], in0=pre[:], scalar1=0.0, scalar2=NOISE_EPS, op0=ALU.max, op1=ALU.add
         )
 
-        regroup_w1_on_vector(0)
-        regroup_w1_on_scalar(0)
-
-        x_words = x_rows[:].bitcast(F32).rearrange("b (p u) -> b u p", u=2)
-        xT_ps = psum_setup.tile([P, 2, B], F32)
-        for u in range(2):
-            nc.tensor.transpose(xT_ps[:, u, :], x_words[:, u, :], ident[:])
-        b1_rows_f32 = consts.tile([P, P], F32)
-        nc.vector.tensor_copy(out=b1_rows_f32[:], in_=b1_rows[:])
-        b1T_ps = psum_setup.tile([P, P], F32)
-        nc.tensor.transpose(b1T_ps[:], b1_rows_f32[:], ident[:])
-        b2_ps = psum_setup.tile([P, E, L], F32)
-        nc.tensor.matmul(
-            b2_ps[:].rearrange("p e l -> p (e l)"), lhsT=ones[:], rhs=b2_row[:], start=True, stop=True
-        )
-
         x_grouped = consts.tile([P, B * PACK], BF16, align_bytes=64)
-        nc.vector.tensor_copy(
-            out=x_grouped[:].bitcast(F32).rearrange("p (b u) -> p b u", u=2),
-            in_=xT_ps[:].rearrange("p u b -> p b u"),
-        )
+        x_codes = consts.tile([P, B], U32, align_bytes=64)
+        x_scales = consts.tile([P, B], U8, align_bytes=64)
+        b1T = consts.tile([P, E * PACK], F32)
+        b2_all = consts.tile([B, E, L], F32)
+        with tc.psum_pool(name="psum_setup", bufs=1) as psum_setup:
+            x_words = x_rows[:].bitcast(F32).rearrange("b (p u) -> b u p", u=2)
+            xT_ps = psum_setup.tile([P, 2, B], F32)
+            for u in range(2):
+                nc.tensor.transpose(xT_ps[:, u, :], x_words[:, u, :], ident[:])
+            b1_rows_f32 = consts.tile([P, P], F32)
+            nc.vector.tensor_copy(out=b1_rows_f32[:], in_=b1_rows[:])
+            b1T_ps = psum_setup.tile([P, P], F32)
+            nc.tensor.transpose(b1T_ps[:], b1_rows_f32[:], ident[:])
+            b2_ps = psum_setup.tile([P, E, L], F32)
+            nc.tensor.matmul(
+                b2_ps[:].rearrange("p e l -> p (e l)"), lhsT=ones[:], rhs=b2_row[:], start=True, stop=True
+            )
+            nc.vector.tensor_copy(
+                out=x_grouped[:].bitcast(F32).rearrange("p (b u) -> p b u", u=2),
+                in_=xT_ps[:].rearrange("p u b -> p b u"),
+            )
+            nc.vector.tensor_copy(out=b1T[:], in_=b1T_ps[:, 0 : E * PACK])
+            nc.vector.tensor_copy(out=b2_all[:], in_=b2_ps[:])
+        nc.vector.quantize_mx(out=x_codes[:].bitcast(FP8X4), scales=x_scales[:], in_=x_grouped[:])
+
+        psum_h = ctx.enter_context(tc.psum_pool(name="psum_h", bufs=PSUM_BANKS - Y_BANKS))
+        psum_y = ctx.enter_context(tc.psum_pool(name="psum_y", bufs=Y_BANKS))
+
+        w1_grouped = {}
+        hT_ps = {}
+
+        def regroup_w1(e):
+            w1_grouped[e] = stage.tile([P, H, PACK], BF16, align_bytes=64, name="w1_grouped")
+            regroup(nc.vector.tensor_copy, w1_grouped[e][:, 0:VECTOR_COLS, :], w1_raw[e][:, :, 0:VECTOR_COLS])
+            regroup(nc.scalar.copy, w1_grouped[e][:, VECTOR_COLS:H, :], w1_raw[e][:, :, VECTOR_COLS:H])
+
+        def first_product(e):
+            w1_codes = per_expert.tile([P, H], U32, align_bytes=64)
+            w1_scales = per_expert.tile([P, H], U8, align_bytes=64)
+            nc.vector.quantize_mx(
+                out=w1_codes[:].bitcast(FP8X4),
+                scales=w1_scales[:],
+                in_=w1_grouped[e][:].rearrange("p h j -> p (h j)"),
+            )
+            hT_ps[e] = psum_h.tile([P, PACK, B], F32, name="hT_ps")
+            for t in range(PACK):
+                cols = slice(t * P, (t + 1) * P)
+                nc.tensor.matmul_mx(
+                    out=hT_ps[e][:, t, :],
+                    lhsT=w1_codes[:, cols].bitcast(FP8X4),
+                    lhsT_scale=w1_scales[:, cols],
+                    rhs=x_codes[:].bitcast(FP8X4),
+                    rhs_scale=x_scales[:],
+                    start=True,
+                    stop=True,
+                )
+
+        regroup_w1(0)
 
         sd = consts.tile([B, E], F32)
         nc.vector.tensor_tensor(out=sd[:], in0=log_pre[:], in1=relu_pre[:], op=ALU.add)
@@ -238,58 +161,104 @@ def tile_mblfe_pa_s_kernel(tc, x, noise, clean_logits, noise_pre, W1, b1, W2, b2
         neg_max = consts.tile([B, 1], F32)
         nc.vector.tensor_scalar_mul(neg_max[:], row_max[:], -1.0)
 
-        nc.vector.tensor_copy(out=b1T[:], in_=b1T_ps[:, 0 : E * PACK])
-        nc.vector.quantize_mx(out=x_codes[:].bitcast(FP8X4), scales=x_scales[:], in_=x_grouped[:])
+        for e in range(1, E):
+            regroup_w1(e)
+            first_product(e - 1)
+        first_product(E - 1)
+
+        w2_grouped = consts.tile([P, E, L, PACK], BF16, align_bytes=64)
+        nc.vector.tensor_copy(out=w2_grouped[:], in_=w2_raw[:].rearrange("p e t l -> p e l t"))
 
         ex = consts.tile([B, E], F32)
         ex_sum = consts.tile([B, 1], F32)
+        nc.scalar.activation(
+            out=ex[:], in_=logits[:], func=ACT.Exp, bias=neg_max[:, 0:1], accum_out=ex_sum[:, 0:1]
+        )
+        threshold = consts.tile([B, 1], F32)
+        nc.vector.tensor_scalar_mul(threshold[:], ex_sum[:], 1.0 / E - MEAN_EPS)
+        kept = consts.tile([B, E], F32)
+        nc.vector.scalar_tensor_tensor(
+            out=kept[:], in0=ex[:], scalar=threshold[:, 0:1], in1=ex[:], op0=ALU.is_ge, op1=ALU.mult
+        )
+        kept_sum = consts.tile([B, 1], F32)
+        nc.vector.reduce_sum(out=kept_sum[:], in_=kept[:], axis=AX.X)
+        inv_sum = consts.tile([B, 1], F32)
+        nc.vector.reciprocal(out=inv_sum[:], in_=kept_sum[:])
+        gates = consts.tile([B, E], F32)
+        nc.vector.tensor_scalar_mul(gates[:], kept[:], inv_sum[:, 0:1])
+        gated_b2 = consts.tile([B, E, L], F32)
+        nc.vector.tensor_tensor(
+            out=gated_b2[:], in0=b2_all[:], in1=gates[:].unsqueeze(2).to_broadcast([B, E, L]), op=ALU.mult
+        )
 
-        def softmax_exponentials():
-            nc.scalar.activation(
-                out=ex[:], in_=logits[:], func=ACT.Exp, bias=neg_max[:, 0:1], accum_out=ex_sum[:, 0:1]
+        w2_codes = consts.tile([P, E * L], U32, align_bytes=64)
+        w2_scales = consts.tile([P, E * L], U8, align_bytes=64)
+        nc.vector.quantize_mx(
+            out=w2_codes[:].bitcast(FP8X4),
+            scales=w2_scales[:],
+            in_=w2_grouped[:].rearrange("p e l t -> p (e l t)"),
+        )
+
+        result = consts.tile([B, E, L], F32)
+        h_planes = {}
+        h_grouped = {}
+        y_ps = {}
+
+        def tanh(e):
+            h_planes[e] = per_expert.tile([P, PACK, B], BF16, name="h_planes")
+            for t in range(PACK):
+                nc.scalar.activation(
+                    out=h_planes[e][:, t, :],
+                    in_=hT_ps[e][:, t, :],
+                    func=ACT.Tanh,
+                    bias=b1T[:, e * PACK + t : e * PACK + t + 1],
+                )
+
+        def regroup_h(e):
+            h_grouped[e] = stage.tile([P, B, PACK], BF16, align_bytes=64, name="h_grouped")
+            regroup(nc.vector.tensor_copy, h_grouped[e][:], h_planes[e][:])
+
+        def second_product(e):
+            h_codes = stage.tile([P, B], U32, align_bytes=64)
+            h_scales = stage.tile([P, B], U8, align_bytes=64)
+            nc.vector.quantize_mx(
+                out=h_codes[:].bitcast(FP8X4),
+                scales=h_scales[:],
+                in_=h_grouped[e][:].rearrange("p b t -> p (b t)"),
+            )
+            window = (e * L) // N_MIN * N_MIN
+            y_ps[e] = psum_y.tile([B, N_MIN], F32, name="y_ps")
+            nc.tensor.matmul_mx(
+                out=y_ps[e][:],
+                lhsT=h_codes[:].bitcast(FP8X4),
+                lhsT_scale=h_scales[:],
+                rhs=w2_codes[:, window : window + N_MIN].bitcast(FP8X4),
+                rhs_scale=w2_scales[:, window : window + N_MIN],
+                start=True,
+                stop=True,
             )
 
-        def gates_from_exponentials():
-            threshold = consts.tile([B, 1], F32)
-            nc.vector.tensor_scalar_mul(threshold[:], ex_sum[:], 1.0 / E - MEAN_EPS)
-            kept = consts.tile([B, E], F32)
+        def finish(e):
+            first = (e * L) % N_MIN
             nc.vector.scalar_tensor_tensor(
-                out=kept[:], in0=ex[:], scalar=threshold[:, 0:1], in1=ex[:], op0=ALU.is_ge, op1=ALU.mult
-            )
-            kept_sum = consts.tile([B, 1], F32)
-            nc.vector.reduce_sum(out=kept_sum[:], in_=kept[:], axis=AX.X)
-            inv_sum = consts.tile([B, 1], F32)
-            nc.vector.reciprocal(out=inv_sum[:], in_=kept_sum[:])
-            nc.vector.tensor_scalar_mul(gates[:], kept[:], inv_sum[:, 0:1])
-            nc.vector.tensor_tensor(
-                out=gated_b2[:], in0=b2_ps[:], in1=gates[:].unsqueeze(2).to_broadcast([B, E, L]), op=ALU.mult
+                out=result[:, e, :],
+                in0=y_ps[e][:, first : first + L],
+                scalar=gates[:, e : e + 1],
+                in1=gated_b2[:, e, :],
+                op0=ALU.mult,
+                op1=ALU.add,
             )
 
         def live(e):
             return 0 <= e < E
 
-        for s in range(1 - REGROUP_AHEAD, E + FINISH_BEHIND):
-            if live(s + REGROUP_AHEAD):
-                regroup_w1_on_vector(s + REGROUP_AHEAD)
-            if live(s - SECOND_BEHIND):
-                regroup_h(s - SECOND_BEHIND)
-            if live(s) and s % E_HALF == 0:
-                regroup_w2(s // E_HALF)
-            if live(s + PRODUCT_AHEAD):
-                first_product(s + PRODUCT_AHEAD)
-            if live(s) and s % E_HALF == 0:
-                quantise_w2(s // E_HALF)
-            if live(s - SECOND_BEHIND):
-                second_product(s - SECOND_BEHIND)
-            if s == FINISH_BEHIND:
-                gates_from_exponentials()
-            if live(s - FINISH_BEHIND):
-                finish(s - FINISH_BEHIND)
-            if s == 0:
-                softmax_exponentials()
+        for s in range(E + FINISH_BEHIND):
             if live(s):
                 tanh(s)
-            if live(s + REGROUP_AHEAD):
-                regroup_w1_on_scalar(s + REGROUP_AHEAD)
+                regroup_h(s)
+            if live(s - FINISH_BEHIND):
+                finish(s - FINISH_BEHIND)
+            if live(s - SECOND_BEHIND):
+                second_product(s - SECOND_BEHIND)
 
         nc.sync.dma_start(out=out, in_=result[:])

@@ -20,7 +20,7 @@ P = 128
 PACK = 4
 N_MIN = 128
 RUN = 4
-VECTOR_COLS = 288
+VECTOR_COLS = 256
 PSUM_BANKS = 8
 Y_BANKS = 2
 

@@ -20,12 +20,12 @@ P = 128
 PACK = 4
 N_MIN = 128
 RUN = 4
-VECTOR_COLS = 256
+VECTOR_COLS = 288
 PSUM_BANKS = 8
 Y_BANKS = 2
+PER_BANK = 4
 
 SECOND_BEHIND = 1
-FINISH_BEHIND = 3
 
 FLOPS = 2 * B * D * H * E + 2 * B * H * L * E
 
@@ -56,10 +56,10 @@ def tile_mblfe_pa_s_kernel(tc, x, noise, clean_logits, noise_pre, W1, b1, W2, b2
 
         pre = consts.tile([B, E], BF16)
         nc.sync.dma_start(out=pre[:], in_=noise_pre)
-        x_rows = consts.tile([B, D], BF16)
-        nc.sync.dma_start(out=x_rows[:], in_=x)
         nc.sync.dma_start(out=b1_rows[0 : E * PACK, :], in_=b1.rearrange("e (t p) -> (e t) p", p=P))
         nc.sync.dma_start(out=b2_row[0:1, :], in_=b2.rearrange("(o e) l -> o (e l)", o=1))
+        x_rows = consts.tile([B, D], BF16)
+        nc.sync.dma_start(out=x_rows[:], in_=x)
         w1_raw = {}
 
         def load_w1(e):
@@ -96,10 +96,6 @@ def tile_mblfe_pa_s_kernel(tc, x, noise, clean_logits, noise_pre, W1, b1, W2, b2
         b1T = consts.tile([P, E * PACK], F32)
         b2_all = consts.tile([B, E, L], F32)
         with tc.psum_pool(name="psum_setup", bufs=1) as psum_setup:
-            x_words = x_rows[:].bitcast(F32).rearrange("b (p u) -> b u p", u=2)
-            xT_ps = psum_setup.tile([P, 2, B], F32)
-            for u in range(2):
-                nc.tensor.transpose(xT_ps[:, u, :], x_words[:, u, :], ident[:])
             b1_rows_f32 = consts.tile([P, P], F32)
             nc.vector.tensor_copy(out=b1_rows_f32[:], in_=b1_rows[:])
             b1T_ps = psum_setup.tile([P, P], F32)
@@ -108,13 +104,16 @@ def tile_mblfe_pa_s_kernel(tc, x, noise, clean_logits, noise_pre, W1, b1, W2, b2
             nc.tensor.matmul(
                 b2_ps[:].rearrange("p e l -> p (e l)"), lhsT=ones[:], rhs=b2_row[:], start=True, stop=True
             )
+            x_words = x_rows[:].bitcast(F32).rearrange("b (p u) -> b u p", u=2)
+            xT_ps = psum_setup.tile([P, 2, B], F32)
+            for u in range(2):
+                nc.tensor.transpose(xT_ps[:, u, :], x_words[:, u, :], ident[:])
+            nc.vector.tensor_copy(out=b1T[:], in_=b1T_ps[:, 0 : E * PACK])
+            nc.vector.tensor_copy(out=b2_all[:], in_=b2_ps[:])
             nc.vector.tensor_copy(
                 out=x_grouped[:].bitcast(F32).rearrange("p (b u) -> p b u", u=2),
                 in_=xT_ps[:].rearrange("p u b -> p b u"),
             )
-            nc.vector.tensor_copy(out=b1T[:], in_=b1T_ps[:, 0 : E * PACK])
-            nc.vector.tensor_copy(out=b2_all[:], in_=b2_ps[:])
-        nc.vector.quantize_mx(out=x_codes[:].bitcast(FP8X4), scales=x_scales[:], in_=x_grouped[:])
 
         psum_h = ctx.enter_context(tc.psum_pool(name="psum_h", bufs=PSUM_BANKS - Y_BANKS))
         psum_y = ctx.enter_context(tc.psum_pool(name="psum_y", bufs=Y_BANKS))
@@ -148,21 +147,26 @@ def tile_mblfe_pa_s_kernel(tc, x, noise, clean_logits, noise_pre, W1, b1, W2, b2
                     stop=True,
                 )
 
-        regroup_w1(0)
-
         sd = consts.tile([B, E], F32)
-        nc.vector.tensor_tensor(out=sd[:], in0=log_pre[:], in1=relu_pre[:], op=ALU.add)
         scaled_noise = consts.tile([B, E], F32)
-        nc.vector.tensor_tensor(out=scaled_noise[:], in0=sd[:], in1=eps_noise[:], op=ALU.mult)
         logits = consts.tile([B, E], F32)
-        nc.vector.tensor_tensor(out=logits[:], in0=scaled_noise[:], in1=clean[:], op=ALU.add)
         row_max = consts.tile([B, 1], F32)
-        nc.vector.reduce_max(out=row_max[:], in_=logits[:], axis=AX.X)
         neg_max = consts.tile([B, 1], F32)
-        nc.vector.tensor_scalar_mul(neg_max[:], row_max[:], -1.0)
+        logit_links = [
+            lambda: nc.vector.tensor_tensor(out=sd[:], in0=log_pre[:], in1=relu_pre[:], op=ALU.add),
+            lambda: nc.vector.tensor_tensor(out=scaled_noise[:], in0=sd[:], in1=eps_noise[:], op=ALU.mult),
+            lambda: nc.vector.tensor_tensor(out=logits[:], in0=scaled_noise[:], in1=clean[:], op=ALU.add),
+            lambda: nc.vector.reduce_max(out=row_max[:], in_=logits[:], axis=AX.X),
+            lambda: nc.vector.tensor_scalar_mul(neg_max[:], row_max[:], -1.0),
+        ]
+        assert len(logit_links) < E
 
+        regroup_w1(0)
+        nc.vector.quantize_mx(out=x_codes[:].bitcast(FP8X4), scales=x_scales[:], in_=x_grouped[:])
         for e in range(1, E):
             regroup_w1(e)
+            if e <= len(logit_links):
+                logit_links[e - 1]()
             first_product(e - 1)
         first_product(E - 1)
 
@@ -175,21 +179,24 @@ def tile_mblfe_pa_s_kernel(tc, x, noise, clean_logits, noise_pre, W1, b1, W2, b2
             out=ex[:], in_=logits[:], func=ACT.Exp, bias=neg_max[:, 0:1], accum_out=ex_sum[:, 0:1]
         )
         threshold = consts.tile([B, 1], F32)
-        nc.vector.tensor_scalar_mul(threshold[:], ex_sum[:], 1.0 / E - MEAN_EPS)
         kept = consts.tile([B, E], F32)
-        nc.vector.scalar_tensor_tensor(
-            out=kept[:], in0=ex[:], scalar=threshold[:, 0:1], in1=ex[:], op0=ALU.is_ge, op1=ALU.mult
-        )
         kept_sum = consts.tile([B, 1], F32)
-        nc.vector.reduce_sum(out=kept_sum[:], in_=kept[:], axis=AX.X)
         inv_sum = consts.tile([B, 1], F32)
-        nc.vector.reciprocal(out=inv_sum[:], in_=kept_sum[:])
         gates = consts.tile([B, E], F32)
-        nc.vector.tensor_scalar_mul(gates[:], kept[:], inv_sum[:, 0:1])
         gated_b2 = consts.tile([B, E, L], F32)
-        nc.vector.tensor_tensor(
-            out=gated_b2[:], in0=b2_all[:], in1=gates[:].unsqueeze(2).to_broadcast([B, E, L]), op=ALU.mult
-        )
+        gate_links = [
+            lambda: nc.vector.tensor_scalar_mul(threshold[:], ex_sum[:], 1.0 / E - MEAN_EPS),
+            lambda: nc.vector.scalar_tensor_tensor(
+                out=kept[:], in0=ex[:], scalar=threshold[:, 0:1], in1=ex[:], op0=ALU.is_ge, op1=ALU.mult
+            ),
+            lambda: nc.vector.reduce_sum(out=kept_sum[:], in_=kept[:], axis=AX.X),
+            lambda: nc.vector.reciprocal(out=inv_sum[:], in_=kept_sum[:]),
+            lambda: nc.vector.tensor_scalar_mul(gates[:], kept[:], inv_sum[:, 0:1]),
+            lambda: nc.vector.tensor_tensor(
+                out=gated_b2[:], in0=b2_all[:], in1=gates[:].unsqueeze(2).to_broadcast([B, E, L]), op=ALU.mult
+            ),
+        ]
+        finish_behind = len(gate_links)
 
         w2_codes = consts.tile([P, E * L], U32, align_bytes=64)
         w2_scales = consts.tile([P, E * L], U8, align_bytes=64)
@@ -227,9 +234,10 @@ def tile_mblfe_pa_s_kernel(tc, x, noise, clean_logits, noise_pre, W1, b1, W2, b2
                 in_=h_grouped[e][:].rearrange("p b t -> p (b t)"),
             )
             window = (e * L) // N_MIN * N_MIN
-            y_ps[e] = psum_y.tile([B, N_MIN], F32, name="y_ps")
+            if e % PER_BANK == 0:
+                y_ps[e // PER_BANK] = psum_y.tile([B, PER_BANK, N_MIN], F32, name="y_ps")
             nc.tensor.matmul_mx(
-                out=y_ps[e][:],
+                out=y_ps[e // PER_BANK][:, e % PER_BANK, :],
                 lhsT=h_codes[:].bitcast(FP8X4),
                 lhsT_scale=h_scales[:],
                 rhs=w2_codes[:, window : window + N_MIN].bitcast(FP8X4),
@@ -242,7 +250,7 @@ def tile_mblfe_pa_s_kernel(tc, x, noise, clean_logits, noise_pre, W1, b1, W2, b2
             first = (e * L) % N_MIN
             nc.vector.scalar_tensor_tensor(
                 out=result[:, e, :],
-                in0=y_ps[e][:, first : first + L],
+                in0=y_ps[e // PER_BANK][:, e % PER_BANK, first : first + L],
                 scalar=gates[:, e : e + 1],
                 in1=gated_b2[:, e, :],
                 op0=ALU.mult,
@@ -252,12 +260,14 @@ def tile_mblfe_pa_s_kernel(tc, x, noise, clean_logits, noise_pre, W1, b1, W2, b2
         def live(e):
             return 0 <= e < E
 
-        for s in range(E + FINISH_BEHIND):
+        for s in range(E + finish_behind):
             if live(s):
                 tanh(s)
                 regroup_h(s)
-            if live(s - FINISH_BEHIND):
-                finish(s - FINISH_BEHIND)
+            if s < len(gate_links):
+                gate_links[s]()
+            if live(s - finish_behind):
+                finish(s - finish_behind)
             if live(s - SECOND_BEHIND):
                 second_product(s - SECOND_BEHIND)
 

from contextlib import ExitStack

import concourse.mybir as mybir
from concourse.masks import make_identity

F32 = mybir.dt.float32
BF16 = mybir.dt.bfloat16
U32 = mybir.dt.uint32
U8 = mybir.dt.uint8
FP8X4 = mybir.dt.float8_e4m3fn_x4
ACT = mybir.ActivationFunctionType
ALU = mybir.AluOpType
AX = mybir.AxisListType

B, D, E, H, L = 128, 512, 8, 512, 32
NOISE_EPS = 0.01
MEAN_EPS = 1e-8

P = 128
PACK = 4
N_MIN = 128
RUN = 4
VECTOR_COLS = 288
PSUM_BANKS = 8
Y_BANKS = 2
PER_BANK = 4

SECOND_BEHIND = 1

FLOPS = 2 * B * D * H * E + 2 * B * H * L * E


def regroup(copy, dst, src):
    copy(
        out=dst.rearrange("p (c i) j -> p c j i", i=RUN),
        in_=src.rearrange("p j (c i) -> p c j i", i=RUN),
    )


def tile_mblfe_pa_s_kernel(tc, x, noise, clean_logits, noise_pre, W1, b1, W2, b2, out):
    nc = tc.nc
    with ExitStack() as ctx:
        ctx.enter_context(tc.manual_schedule())
        consts = ctx.enter_context(tc.tile_pool(name="consts", bufs=1))
        per_expert = ctx.enter_context(tc.tile_pool(name="per_expert", bufs=E))
        stage = ctx.enter_context(tc.tile_pool(name="stage", bufs=3))

        b1_rows = consts.tile([P, P], BF16)
        nc.vector.memset(b1_rows[:], 0.0)
        b2_row = consts.tile([P, E * L], BF16)
        nc.vector.memset(b2_row[:], 0.0)
        ones = consts.tile([P, P], BF16)
        nc.vector.memset(ones[:], 1.0)
        one_col = consts.tile([P, 1], F32)
        nc.vector.memset(one_col[:], 1.0)

        pre = consts.tile([B, E], BF16)
        nc.sync.dma_start(out=pre[:], in_=noise_pre)
        nc.sync.dma_start(out=b1_rows[0 : E * PACK, :], in_=b1.rearrange("e (t p) -> (e t) p", p=P))
        nc.sync.dma_start(out=b2_row[0:1, :], in_=b2.rearrange("(o e) l -> o (e l)", o=1))
        x_rows = consts.tile([B, D], BF16)
        nc.sync.dma_start(out=x_rows[:], in_=x)
        w1_raw = {}

        def load_w1(e):
            w1_raw[e] = per_expert.tile([P, PACK, H], BF16, name="w1_raw")
            nc.sync.dma_start(out=w1_raw[e][:], in_=W1[e].rearrange("(p j) h -> p j h", j=PACK))

        load_w1(0)
        eps_noise = consts.tile([B, E], BF16)
        nc.sync.dma_start(out=eps_noise[:], in_=noise)
        clean = consts.tile([B, E], BF16)
        nc.sync.dma_start(out=clean[:], in_=clean_logits)
        for e in range(1, E):
            load_w1(e)
        w2_raw = consts.tile([P, E, PACK, L], BF16)
        nc.sync.dma_start(out=w2_raw[:], in_=W2.rearrange("e (t p) l -> p e t l", p=P))

        ident = consts.tile([P, P], F32)
        make_identity(nc, ident[:])

        abs_pre = consts.tile([B, E], F32)
        nc.scalar.activation(out=abs_pre[:], in_=pre[:], func=ACT.Abs)
        exp_pre = consts.tile([B, E], F32)
        nc.scalar.activation(out=exp_pre[:], in_=abs_pre[:], func=ACT.Exp, scale=-1.0)
        log_pre = consts.tile([B, E], F32)
        nc.scalar.activation(out=log_pre[:], in_=exp_pre[:], func=ACT.Ln, bias=one_col[:, 0:1])
        relu_pre = consts.tile([B, E], F32)
        nc.vector.tensor_scalar(
            out=relu_pre[:], in0=pre[:], scalar1=0.0, scalar2=NOISE_EPS, op0=ALU.max, op1=ALU.add
        )

        x_grouped = consts.tile([P, B * PACK], BF16, align_bytes=64)
        x_codes = consts.tile([P, B], U32, align_bytes=64)
        x_scales = consts.tile([P, B], U8, align_bytes=64)
        b1T = consts.tile([P, E * PACK], F32)
        b2_all = consts.tile([B, E, L], F32)
        with tc.psum_pool(name="psum_setup", bufs=1) as psum_setup:
            b1_rows_f32 = consts.tile([P, P], F32)
            nc.vector.tensor_copy(out=b1_rows_f32[:], in_=b1_rows[:])
            b1T_ps = psum_setup.tile([P, P], F32)
            nc.tensor.transpose(b1T_ps[:], b1_rows_f32[:], ident[:])
            b2_ps = psum_setup.tile([P, E, L], F32)
            nc.tensor.matmul(
                b2_ps[:].rearrange("p e l -> p (e l)"), lhsT=ones[:], rhs=b2_row[:], start=True, stop=True
            )
            x_words = x_rows[:].bitcast(F32).rearrange("b (p u) -> b u p", u=2)
            xT_ps = psum_setup.tile([P, 2, B], F32)
            for u in range(2):
                nc.tensor.transpose(xT_ps[:, u, :], x_words[:, u, :], ident[:])
            nc.vector.tensor_copy(out=b1T[:], in_=b1T_ps[:, 0 : E * PACK])
            nc.vector.tensor_copy(out=b2_all[:], in_=b2_ps[:])
            nc.vector.tensor_copy(
                out=x_grouped[:].bitcast(F32).rearrange("p (b u) -> p b u", u=2),
                in_=xT_ps[:].rearrange("p u b -> p b u"),
            )

        psum_h = ctx.enter_context(tc.psum_pool(name="psum_h", bufs=PSUM_BANKS - Y_BANKS))
        psum_y = ctx.enter_context(tc.psum_pool(name="psum_y", bufs=Y_BANKS))

        w1_grouped = {}
        hT_ps = {}

        def regroup_w1(e):
            w1_grouped[e] = stage.tile([P, H, PACK], BF16, align_bytes=64, name="w1_grouped")
            regroup(nc.vector.tensor_copy, w1_grouped[e][:, 0:VECTOR_COLS, :], w1_raw[e][:, :, 0:VECTOR_COLS])
            regroup(nc.scalar.copy, w1_grouped[e][:, VECTOR_COLS:H, :], w1_raw[e][:, :, VECTOR_COLS:H])

        def first_product(e):
            w1_codes = per_expert.tile([P, H], U32, align_bytes=64)
            w1_scales = per_expert.tile([P, H], U8, align_bytes=64)
            nc.vector.quantize_mx(
                out=w1_codes[:].bitcast(FP8X4),
                scales=w1_scales[:],
                in_=w1_grouped[e][:].rearrange("p h j -> p (h j)"),
            )
            hT_ps[e] = psum_h.tile([P, PACK, B], F32, name="hT_ps")
            for t in range(PACK):
                cols = slice(t * P, (t + 1) * P)
                nc.tensor.matmul_mx(
                    out=hT_ps[e][:, t, :],
                    lhsT=w1_codes[:, cols].bitcast(FP8X4),
                    lhsT_scale=w1_scales[:, cols],
                    rhs=x_codes[:].bitcast(FP8X4),
                    rhs_scale=x_scales[:],
                    start=True,
                    stop=True,
                )

        sd = consts.tile([B, E], F32)
        scaled_noise = consts.tile([B, E], F32)
        logits = consts.tile([B, E], F32)
        row_max = consts.tile([B, 1], F32)
        neg_max = consts.tile([B, 1], F32)
        logit_links = [
            lambda: nc.vector.tensor_tensor(out=sd[:], in0=log_pre[:], in1=relu_pre[:], op=ALU.add),
            lambda: nc.vector.tensor_tensor(out=scaled_noise[:], in0=sd[:], in1=eps_noise[:], op=ALU.mult),
            lambda: nc.vector.tensor_tensor(out=logits[:], in0=scaled_noise[:], in1=clean[:], op=ALU.add),
            lambda: nc.vector.reduce_max(out=row_max[:], in_=logits[:], axis=AX.X),
            lambda: nc.vector.tensor_scalar_mul(neg_max[:], row_max[:], -1.0),
        ]
        assert len(logit_links) < E

        regroup_w1(0)
        nc.vector.quantize_mx(out=x_codes[:].bitcast(FP8X4), scales=x_scales[:], in_=x_grouped[:])
        for e in range(1, E):
            regroup_w1(e)
            if e <= len(logit_links):
                logit_links[e - 1]()
            first_product(e - 1)
        first_product(E - 1)

        w2_grouped = consts.tile([P, E, L, PACK], BF16, align_bytes=64)
        nc.vector.tensor_copy(out=w2_grouped[:], in_=w2_raw[:].rearrange("p e t l -> p e l t"))

        ex = consts.tile([B, E], F32)
        ex_sum = consts.tile([B, 1], F32)
        nc.scalar.activation(
            out=ex[:], in_=logits[:], func=ACT.Exp, bias=neg_max[:, 0:1], accum_out=ex_sum[:, 0:1]
        )
        threshold = consts.tile([B, 1], F32)
        kept = consts.tile([B, E], F32)
        kept_sum = consts.tile([B, 1], F32)
        inv_sum = consts.tile([B, 1], F32)
        gates = consts.tile([B, E], F32)
        gated_b2 = consts.tile([B, E, L], F32)
        gate_links = [
            lambda: nc.vector.tensor_scalar_mul(threshold[:], ex_sum[:], 1.0 / E - MEAN_EPS),
            lambda: nc.vector.scalar_tensor_tensor(
                out=kept[:], in0=ex[:], scalar=threshold[:, 0:1], in1=ex[:], op0=ALU.is_ge, op1=ALU.mult
            ),
            lambda: nc.vector.reduce_sum(out=kept_sum[:], in_=kept[:], axis=AX.X),
            lambda: nc.vector.reciprocal(out=inv_sum[:], in_=kept_sum[:]),
            lambda: nc.vector.tensor_scalar_mul(gates[:], kept[:], inv_sum[:, 0:1]),
            lambda: nc.vector.tensor_tensor(
                out=gated_b2[:], in0=b2_all[:], in1=gates[:].unsqueeze(2).to_broadcast([B, E, L]), op=ALU.mult
            ),
        ]
        finish_behind = len(gate_links)

        w2_codes = consts.tile([P, E * L], U32, align_bytes=64)
        w2_scales = consts.tile([P, E * L], U8, align_bytes=64)
        nc.vector.quantize_mx(
            out=w2_codes[:].bitcast(FP8X4),
            scales=w2_scales[:],
            in_=w2_grouped[:].rearrange("p e l t -> p (e l t)"),
        )

        result = consts.tile([B, E, L], F32)
        h_planes = {}
        h_grouped = {}
        y_ps = {}

        def tanh(e):
            h_planes[e] = per_expert.tile([P, PACK, B], BF16, name="h_planes")
            for t in range(PACK):
                nc.scalar.activation(
                    out=h_planes[e][:, t, :],
                    in_=hT_ps[e][:, t, :],
                    func=ACT.Tanh,
                    bias=b1T[:, e * PACK + t : e * PACK + t + 1],
                )

        def regroup_h(e):
            h_grouped[e] = stage.tile([P, B, PACK], BF16, align_bytes=64, name="h_grouped")
            regroup(nc.vector.tensor_copy, h_grouped[e][:], h_planes[e][:])

        def second_product(e):
            h_codes = stage.tile([P, B], U32, align_bytes=64)
            h_scales = stage.tile([P, B], U8, align_bytes=64)
            nc.vector.quantize_mx(
                out=h_codes[:].bitcast(FP8X4),
                scales=h_scales[:],
                in_=h_grouped[e][:].rearrange("p b t -> p (b t)"),
            )
            window = (e * L) // N_MIN * N_MIN
            if e % PER_BANK == 0:
                y_ps[e // PER_BANK] = psum_y.tile([B, PER_BANK, N_MIN], F32, name="y_ps")
            nc.tensor.matmul_mx(
                out=y_ps[e // PER_BANK][:, e % PER_BANK, :],
                lhsT=h_codes[:].bitcast(FP8X4),
                lhsT_scale=h_scales[:],
                rhs=w2_codes[:, window : window + N_MIN].bitcast(FP8X4),
                rhs_scale=w2_scales[:, window : window + N_MIN],
                start=True,
                stop=True,
            )

        def finish(e):
            first = (e * L) % N_MIN
            nc.vector.scalar_tensor_tensor(
                out=result[:, e, :],
                in0=y_ps[e // PER_BANK][:, e % PER_BANK, first : first + L],
                scalar=gates[:, e : e + 1],
                in1=gated_b2[:, e, :],
                op0=ALU.mult,
                op1=ALU.add,
            )

        def live(e):
            return 0 <= e < E

        for s in range(E + finish_behind):
            if live(s):
                tanh(s)
                regroup_h(s)
            if s < len(gate_links):
                gate_links[s]()
            if live(s - finish_behind):
                finish(s - finish_behind)
            if live(s - SECOND_BEHIND):
                second_product(s - SECOND_BEHIND)

        nc.sync.dma_start(out=out, in_=result[:])
